import numpy as np
import ml_dtypes


def mxq(x, axis, fmt="e4m3"):
    dtype, down = {"e4m3": (ml_dtypes.float8_e4m3fn, 7), "e5m2": (ml_dtypes.float8_e5m2, 14)}[fmt]
    v = np.moveaxis(np.asarray(x, np.float32).astype(ml_dtypes.bfloat16).astype(np.float64), axis, -1)
    blocks = v.reshape(v.shape[:-1] + (-1, 32))
    amax = np.abs(blocks).max(-1, keepdims=True)
    byte = np.maximum(np.where(amax > 0, np.frexp(amax)[1] - 1 + 127, 0) - down, 1)
    scale = np.exp2(byte - 127.0)
    codes = (blocks / scale).astype(np.float32).astype(dtype).astype(np.float64)
    return np.moveaxis((codes * scale).reshape(v.shape), -1, axis)


WIDE = False


def mx_kscale(k):
    if not WIDE:
        return np.ones(k)
    levels = np.array([10, -10, 5, -5, 0])
    a = np.random.permutation(np.resize(levels, k // 512 * 4)).reshape(k // 512, 4)
    idx = np.arange(k)
    return np.exp2(a[idx // 512, idx % 128 // 32])


BF16 = ml_dtypes.bfloat16


def bf(x):
    return np.asarray(x, np.float32).astype(BF16)


def f64(x):
    return np.asarray(x).astype(np.float64)


B, S, D, F, P, NQ = 4, 2048, 512, 128, 1024, 3
GATE_EPS = 1e-9


def silu(v):
    return v / (1.0 + np.exp(-v))


def setup_inputs():
    s = mx_kscale(D)
    return {"h_ln": bf(np.random.standard_normal((B, S, D)) * s),
            "mu_w": bf(np.random.standard_normal((NQ, F, D)) * 2.0 / np.sqrt(D) / s),
            "mu_b": bf(np.random.standard_normal((NQ, F)) * 0.3),
            "proto_state": bf(np.random.standard_normal((NQ, F, D)) * 1.1 / s),
            "gate": bf(np.random.standard_normal((NQ, F)) * 0.5)}


def reference(h_ln, mu_w, mu_b, proto_state, gate):
    hq = mxq(f64(h_ln).reshape(B * S, D), 1, "e4m3")
    comp = silu((hq @ mxq(f64(mu_w), 2, "e4m3").transpose(0, 2, 1)) + f64(mu_b)[:, None, :])
    mv = (hq @ mxq(f64(proto_state), 2, "e4m3").transpose(0, 2, 1)) * (1.0 / np.sqrt(D))
    g = f64(gate)
    cost = g / (np.max(np.abs(g), axis=-1, keepdims=True) + GATE_EPS)
    logits = mv - cost[:, None, :]
    return (comp * (logits > 0)).reshape(NQ, B, S, F)

@@ -1,0 +1,184 @@
+from contextlib import ExitStack
+import math
+
+import concourse.mybir as mybir
+from concourse.masks import make_identity
+
+F32 = mybir.dt.float32
+BF16 = mybir.dt.bfloat16
+U32 = mybir.dt.uint32
+U8 = mybir.dt.uint8
+FP8X4 = mybir.dt.float8_e4m3fn_x4
+ACT = mybir.ActivationFunctionType
+ALU = mybir.AluOpType
+AX = mybir.AxisListType
+
+P = 128
+TOKENS = 8192
+D = 512
+WORDS = D // 2
+F = 128
+NQ = 3
+BLOCK = 512
+SUB = BLOCK // P
+NB = TOKENS // BLOCK
+GATE_EPS = 1e-9
+
+FLOPS = 2 * TOKENS * D * 2 * NQ * F
+
+
+def tile_moietransformerblock_pa_t_kernel(tc, h_ln, mu_w, mu_b, proto_state, gate, out):
+    nc = tc.nc
+    h_blocks = h_ln.rearrange("a s k -> (a s) k").rearrange("(b p j) k -> b p (j k)", p=P, j=SUB)
+    out_blocks = out.rearrange("n a s f -> n (a s) f").rearrange("n (b p j) f -> b p n (j f)", p=P, j=SUB)
+
+    with ExitStack() as ctx:
+        const = ctx.enter_context(tc.tile_pool(name="const", bufs=1))
+        xs = ctx.enter_context(tc.tile_pool(name="xs", bufs=NB))
+        work = ctx.enter_context(tc.tile_pool(name="work", bufs=3))
+        acts = ctx.enter_context(tc.tile_pool(name="acts", bufs=6))
+        outs = ctx.enter_context(tc.tile_pool(name="outs", bufs=8))
+        psum = ctx.enter_context(tc.psum_pool(name="psum", bufs=8))
+        ctx.enter_context(tc.manual_schedule())
+
+        small = const.tile([P, 2 * F], BF16)
+        nc.vector.memset(small[:], 0.0)
+        nc.scalar.dma_start(out=small[0:NQ, 0:F], in_=gate)
+        nc.scalar.dma_start(out=small[0:NQ, F:2 * F], in_=mu_b)
+        w_raw = const.tile([P, 2 * NQ * D], BF16)
+        nc.sync.dma_start(out=w_raw[:, 0:NQ * D].rearrange("f (n k) -> f n k", n=NQ),
+                          in_=mu_w.rearrange("n f k -> f n k"))
+        nc.sync.dma_start(out=w_raw[:, NQ * D:2 * NQ * D].rearrange("f (n k) -> f n k", n=NQ),
+                          in_=proto_state.rearrange("n f k -> f n k"))
+        x_raw = []
+        for b in range(NB):
+            x_t = xs.tile([P, SUB * D], BF16, tag="x", name="x%d" % b)
+            nc.sync.dma_start(out=x_t[:], in_=h_blocks[b])
+            x_raw.append(x_t)
+
+        ident = const.tile([P, P], F32)
+        make_identity(nc, ident[:])
+        warm = const.tile([P, 2], F32)
+        nc.vector.memset(warm[:], 0.0)
+        nc.scalar.activation(out=warm[:, 1:2], in_=warm[:, 0:1], func=ACT.Silu)
+
+        def flip(src_words, first):
+            bank = psum.tile([P, 2, 2 * P], F32, tag="bank", name="flip")
+            for r in range(2):
+                for u in range(2):
+                    lo = (first + r) * WORDS + u * P
+                    nc.tensor.transpose(bank[:, u, r * P:(r + 1) * P], src_words[:, lo:lo + P], ident[:])
+            return bank
+
+        def regroup(engine_copy, grouped, half, bank):
+            dst = grouped[:].bitcast(F32).rearrange("p (c u) -> p c u", u=2)
+            engine_copy(out=dst[:, half * 2 * P:(half + 1) * 2 * P, :], in_=bank[:].rearrange("p u c -> p c u"))
+
+        rows = const.tile([P, 2 * F], F32)
+        nc.vector.tensor_copy(out=rows[:], in_=small[:])
+        neg = const.tile([P, F], F32)
+        nc.vector.tensor_scalar_mul(out=neg[:], in0=rows[:, 0:F], scalar1=-1.0)
+        nc.vector.tensor_max(out=neg[:], in0=neg[:], in1=rows[:, 0:F])
+        top = const.tile([P, 1], F32)
+        nc.vector.reduce_max(out=top[:], in_=neg[:], axis=AX.X)
+        nc.vector.tensor_scalar_add(out=top[:], in0=top[:], scalar1=GATE_EPS)
+        inv = const.tile([P, 1], F32)
+        nc.vector.reciprocal(out=inv[:], in_=top[:])
+        nc.vector.tensor_scalar(out=rows[:, 0:F], in0=rows[:, 0:F], scalar1=inv[:, 0:1], scalar2=math.sqrt(D),
+                                op0=ALU.mult, op1=ALU.mult)
+
+        w_words = w_raw[:].bitcast(F32)
+        w_grouped = const.tile([P, 2 * NQ * F * 4], BF16, align_bytes=64)
+        w_codes = const.tile([P, 2 * NQ * F], U32, align_bytes=64)
+        w_scales = const.tile([P, 2 * NQ * F], U8, align_bytes=64)
+        for t in range(NQ):
+            bank = flip(w_words, 2 * t)
+            regroup(nc.scalar.copy if t != 1 else nc.vector.tensor_copy, w_grouped, t, bank)
+        nc.vector.quantize_mx(out=w_codes[:, 0:512].bitcast(FP8X4), scales=w_scales[:, 0:512],
+                              in_=w_grouped[:, 0:2048])
+        nc.vector.quantize_mx(out=w_codes[:, 512:768].bitcast(FP8X4), scales=w_scales[:, 512:768],
+                              in_=w_grouped[:, 2048:3072])
+
+        cbank = psum.tile([P, 2, P], F32, tag="bank", name="cbank")
+        for u in range(2):
+            nc.tensor.transpose(cbank[:, u, :], rows[:, u * F:(u + 1) * F], ident[:])
+        percol = const.tile([P, 2, NQ], F32)
+        nc.vector.tensor_copy(out=percol[:], in_=cbank[:, :, 0:NQ])
+
+        st = {}
+
+        def ti(b, h):
+            st["in", b, h] = flip(x_raw[b][:].bitcast(F32), 2 * h)
+
+        def ic(b, h):
+            if h == 0:
+                st["g", b] = work.tile([P, BLOCK * 4], BF16, tag="g", name="g", align_bytes=64)
+            regroup(nc.scalar.copy, st["g", b], h, st["in", b, h])
+
+        def quant(b):
+            codes = work.tile([P, BLOCK], U32, tag="codes", name="codes", align_bytes=64)
+            scales = work.tile([P, BLOCK], U8, tag="scales", name="scales", align_bytes=64)
+            nc.vector.quantize_mx(out=codes[:].bitcast(FP8X4), scales=scales[:], in_=st["g", b][:])
+            st["q", b] = (codes, scales)
+
+        def mx(b, i):
+            codes, scales = st["q", b]
+            acc = psum.tile([P, BLOCK], F32, tag="bank", name="acc")
+            nc.tensor.matmul_mx(out=acc[:], lhsT=w_codes[:, i * F:(i + 1) * F].bitcast(FP8X4),
+                                lhsT_scale=w_scales[:, i * F:(i + 1) * F],
+                                rhs=codes[:].bitcast(FP8X4), rhs_scale=scales[:], start=True, stop=True)
+            st["acc", b, i] = acc
+
+        def silu(b, n):
+            comp = acts.tile([P, BLOCK], F32, tag="comp", name="comp")
+            nc.scalar.activation(out=comp[:], in_=st["acc", b, n][:], func=ACT.Silu,
+                                 bias=percol[:, 1, n:n + 1], scale=1.0)
+            st["comp", b, n] = comp
+
+        def gatemul(b, n):
+            res = acts.tile([P, BLOCK], F32, tag="res", name="res")
+            nc.vector.scalar_tensor_tensor(out=res[:], in0=st["acc", b, NQ + n][:], scalar=percol[:, 0, n:n + 1],
+                                           in1=st["comp", b, n][:], op0=ALU.is_gt, op1=ALU.mult)
+            st["res", b, n] = res
+
+        def to(b, n):
+            bank = psum.tile([P, SUB, F], F32, tag="bank", name="back")
+            for j in range(SUB):
+                nc.tensor.transpose(bank[:, j, :], st["res", b, n][:, j * P:(j + 1) * P], ident[:])
+            st["back", b, n] = bank
+
+        def oc(b, n, engine_copy):
+            o_t = outs.tile([P, SUB * F], F32, tag="o", name="o")
+            engine_copy(out=o_t[:], in_=st["back", b, n][:].rearrange("p j f -> p (j f)"))
+            nc.sync.dma_start(out=out_blocks[b, :, n, :], in_=o_t[:])
+
+        def ok(b):
+            return 0 <= b < NB
+
+        for p in range(-2, NB + 1):
+            if ok(p + 1):
+                ic(p + 1, 0)
+                ic(p + 1, 1)
+                quant(p + 1)
+            if ok(p):
+                for i in (0, 1, NQ, NQ + 1, 2, NQ + 2):
+                    mx(p, i)
+                for n in range(NQ):
+                    silu(p, n)
+                for n in range(NQ):
+                    gatemul(p, n)
+            if ok(p - 1):
+                to(p - 1, 2)
+            if ok(p + 2):
+                ti(p + 2, 0)
+            if ok(p):
+                to(p, 0)
+            if ok(p + 2):
+                ti(p + 2, 1)
+            if ok(p):
+                to(p, 1)
+            if ok(p - 1):
+                oc(p - 1, 2, nc.scalar.copy)
+            if ok(p):
+                oc(p, 0, nc.vector.tensor_copy)
+                oc(p, 1, nc.vector.tensor_copy)

@@ -26,38 +26,56 @@ GATE_EPS = 1e-9
 
 FLOPS = 2 * TOKENS * D * 2 * NQ * F
 
+W_ORDER = ((0, 0), (1, 0), (0, 1), (1, 1), (2, 0), (2, 1))
+
 
 def tile_moietransformerblock_pa_t_kernel(tc, h_ln, mu_w, mu_b, proto_state, gate, out):
     nc = tc.nc
     h_blocks = h_ln.rearrange("a s k -> (a s) k").rearrange("(b p j) k -> b p (j k)", p=P, j=SUB)
     out_blocks = out.rearrange("n a s f -> n (a s) f").rearrange("n (b p j) f -> b p n (j f)", p=P, j=SUB)
+    w_slot = {}
+    for slot, key in enumerate(W_ORDER):
+        w_slot[key] = slot
 
     with ExitStack() as ctx:
         const = ctx.enter_context(tc.tile_pool(name="const", bufs=1))
         xs = ctx.enter_context(tc.tile_pool(name="xs", bufs=NB))
         work = ctx.enter_context(tc.tile_pool(name="work", bufs=3))
-        acts = ctx.enter_context(tc.tile_pool(name="acts", bufs=6))
+        acts = ctx.enter_context(tc.tile_pool(name="acts", bufs=4))
         outs = ctx.enter_context(tc.tile_pool(name="outs", bufs=8))
         psum = ctx.enter_context(tc.psum_pool(name="psum", bufs=8))
         ctx.enter_context(tc.manual_schedule())
 
-        small = const.tile([P, 2 * F], BF16)
-        nc.vector.memset(small[:], 0.0)
-        nc.scalar.dma_start(out=small[0:NQ, 0:F], in_=gate)
-        nc.scalar.dma_start(out=small[0:NQ, F:2 * F], in_=mu_b)
+        row_all = const.tile([P, 2 * NQ * F], BF16)
+        nc.vector.memset(row_all[:], 0.0)
+        row_a = const.tile([P, F], BF16)
+        nc.vector.memset(row_a[:], 0.0)
+        nc.scalar.dma_start(out=row_all[0:1, 0:NQ * F], in_=gate.rearrange("(o n) f -> o (n f)", o=1))
+        nc.scalar.dma_start(out=row_all[0:1, NQ * F:2 * NQ * F], in_=mu_b.rearrange("(o n) f -> o (n f)", o=1))
+        nc.scalar.dma_start(out=row_a[0:1, :], in_=gate[0:1, :])
+        nc.scalar.dma_start(out=row_a[1:2, :], in_=mu_b[0:1, :])
+
         w_raw = const.tile([P, 2 * NQ * D], BF16)
-        nc.sync.dma_start(out=w_raw[:, 0:NQ * D].rearrange("f (n k) -> f n k", n=NQ),
-                          in_=mu_w.rearrange("n f k -> f n k"))
-        nc.sync.dma_start(out=w_raw[:, NQ * D:2 * NQ * D].rearrange("f (n k) -> f n k", n=NQ),
-                          in_=proto_state.rearrange("n f k -> f n k"))
         x_raw = []
         for b in range(NB):
-            x_t = xs.tile([P, SUB * D], BF16, tag="x", name="x%d" % b)
-            nc.sync.dma_start(out=x_t[:], in_=h_blocks[b])
-            x_raw.append(x_t)
+            x_raw.append(xs.tile([P, SUB * D], BF16, tag="x", name="x%d" % b))
+
+        def load_w(src, lo, hi, slot):
+            nc.sync.dma_start(out=w_raw[:, slot * D:(slot + hi - lo) * D].rearrange("f (n k) -> f n k", k=D),
+                              in_=src[lo:hi].rearrange("n f k -> f n k"))
+
+        load_w(mu_w, 0, 2, 0)
+        nc.sync.dma_start(out=x_raw[0][:], in_=h_blocks[0])
+        load_w(proto_state, 0, 2, 2)
+        load_w(mu_w, 2, 3, 4)
+        load_w(proto_state, 2, 3, 5)
+        for b in range(1, NB):
+            nc.sync.dma_start(out=x_raw[b][:], in_=h_blocks[b])
 
         ident = const.tile([P, P], F32)
         make_identity(nc, ident[:])
+        ident_bf = const.tile([P, P], BF16)
+        make_identity(nc, ident_bf[:])
         warm = const.tile([P, 2], F32)
         nc.vector.memset(warm[:], 0.0)
         nc.scalar.activation(out=warm[:, 1:2], in_=warm[:, 0:1], func=ACT.Silu)
@@ -74,36 +92,50 @@ def tile_moietransformerblock_pa_t_kernel(tc, h_ln, mu_w, mu_b, proto_state, gat
             dst = grouped[:].bitcast(F32).rearrange("p (c u) -> p c u", u=2)
             engine_copy(out=dst[:, half * 2 * P:(half + 1) * 2 * P, :], in_=bank[:].rearrange("p u c -> p c u"))
 
-        rows = const.tile([P, 2 * F], F32)
-        nc.vector.tensor_copy(out=rows[:], in_=small[:])
-        neg = const.tile([P, F], F32)
-        nc.vector.tensor_scalar_mul(out=neg[:], in0=rows[:, 0:F], scalar1=-1.0)
-        nc.vector.tensor_max(out=neg[:], in0=neg[:], in1=rows[:, 0:F])
-        top = const.tile([P, 1], F32)
-        nc.vector.reduce_max(out=top[:], in_=neg[:], axis=AX.X)
-        nc.vector.tensor_scalar_add(out=top[:], in0=top[:], scalar1=GATE_EPS)
-        inv = const.tile([P, 1], F32)
-        nc.vector.reciprocal(out=inv[:], in_=top[:])
-        nc.vector.tensor_scalar(out=rows[:, 0:F], in0=rows[:, 0:F], scalar1=inv[:, 0:1], scalar2=math.sqrt(D),
-                                op0=ALU.mult, op1=ALU.mult)
+        first_row = ident_bf[:, 0:1].to_broadcast([P, P])
+        ca_ps = psum.tile([P, 4 * F], F32, tag="bank", name="ca_ps")
+        nc.tensor.matmul(out=ca_ps[:], lhsT=first_row, rhs=row_all[:, 0:4 * F], start=True, stop=True)
+        cb_ps = psum.tile([P, 4 * F], F32, tag="bank", name="cb_ps")
+        nc.tensor.matmul(out=cb_ps[:, 0:2 * F], lhsT=first_row, rhs=row_all[:, 4 * F:6 * F], start=True, stop=True)
+        nc.tensor.matmul(out=cb_ps[:, 2 * F:2 * F + 64], lhsT=row_a[:], rhs=ident_bf[:, 0:64], start=True, stop=True)
 
         w_words = w_raw[:].bitcast(F32)
         w_grouped = const.tile([P, 2 * NQ * F * 4], BF16, align_bytes=64)
         w_codes = const.tile([P, 2 * NQ * F], U32, align_bytes=64)
         w_scales = const.tile([P, 2 * NQ * F], U8, align_bytes=64)
-        for t in range(NQ):
-            bank = flip(w_words, 2 * t)
-            regroup(nc.scalar.copy if t != 1 else nc.vector.tensor_copy, w_grouped, t, bank)
-        nc.vector.quantize_mx(out=w_codes[:, 0:512].bitcast(FP8X4), scales=w_scales[:, 0:512],
-                              in_=w_grouped[:, 0:2048])
-        nc.vector.quantize_mx(out=w_codes[:, 512:768].bitcast(FP8X4), scales=w_scales[:, 512:768],
-                              in_=w_grouped[:, 2048:3072])
+        w_banks = {}
 
-        cbank = psum.tile([P, 2, P], F32, tag="bank", name="cbank")
-        for u in range(2):
-            nc.tensor.transpose(cbank[:, u, :], rows[:, u * F:(u + 1) * F], ident[:])
-        percol = const.tile([P, 2, NQ], F32)
-        nc.vector.tensor_copy(out=percol[:], in_=cbank[:, :, 0:NQ])
+        def wf(t):
+            w_banks[t] = flip(w_words, 2 * t)
+
+        def wc(t, engine_copy):
+            regroup(engine_copy, w_grouped, t, w_banks[t])
+
+        def wq(t):
+            nc.vector.quantize_mx(out=w_codes[:, t * 256:(t + 1) * 256].bitcast(FP8X4),
+                                  scales=w_scales[:, t * 256:(t + 1) * 256],
+                                  in_=w_grouped[:, t * 1024:(t + 1) * 1024])
+
+        wf(0)
+        wc(0, nc.scalar.copy)
+
+        ca = const.tile([P, 4 * F], F32)
+        nc.vector.tensor_copy(out=ca[:], in_=ca_ps[:])
+        cb = const.tile([P, 2 * F + 64], F32)
+        nc.vector.tensor_copy(out=cb[:], in_=cb_ps[:, 0:2 * F + 64])
+        mag = const.tile([P, NQ, F], F32)
+        nc.vector.tensor_scalar_mul(out=mag[:].rearrange("p n f -> p (n f)"), in0=ca[:, 0:NQ * F], scalar1=-1.0)
+        nc.vector.tensor_max(out=mag[:].rearrange("p n f -> p (n f)"), in0=mag[:].rearrange("p n f -> p (n f)"),
+                             in1=ca[:, 0:NQ * F])
+        cs = const.tile([P, NQ], F32)
+        nc.vector.reduce_max(out=cs[:], in_=mag[:], axis=AX.X)
+        nc.vector.tensor_scalar(out=cs[:], in0=cs[:], scalar1=GATE_EPS, scalar2=1.0 / math.sqrt(D),
+                                op0=ALU.add, op1=ALU.mult)
+        thr0 = const.tile([P, 1], F32)
+        nc.vector.reciprocal(out=thr0[:], in_=cs[:, 0:1])
+        nc.vector.tensor_mul(out=thr0[:], in0=thr0[:], in1=cb[:, 2 * F:2 * F + 1])
+        bias0 = cb[:, 2 * F + 1:2 * F + 2]
+        wq(0)
 
         st = {}
 
@@ -121,64 +153,120 @@ def tile_moietransformerblock_pa_t_kernel(tc, h_ln, mu_w, mu_b, proto_state, gat
             nc.vector.quantize_mx(out=codes[:].bitcast(FP8X4), scales=scales[:], in_=st["g", b][:])
             st["q", b] = (codes, scales)
 
-        def mx(b, i):
+        def mx_a(b, kind):
             codes, scales = st["q", b]
+            s = w_slot[0, kind]
             acc = psum.tile([P, BLOCK], F32, tag="bank", name="acc")
-            nc.tensor.matmul_mx(out=acc[:], lhsT=w_codes[:, i * F:(i + 1) * F].bitcast(FP8X4),
-                                lhsT_scale=w_scales[:, i * F:(i + 1) * F],
+            nc.tensor.matmul_mx(out=acc[:], lhsT=w_codes[:, s * F:(s + 1) * F].bitcast(FP8X4),
+                                lhsT_scale=w_scales[:, s * F:(s + 1) * F],
                                 rhs=codes[:].bitcast(FP8X4), rhs_scale=scales[:], start=True, stop=True)
-            st["acc", b, i] = acc
+            st["acc", b, 0, kind] = acc
 
-        def silu(b, n):
-            comp = acts.tile([P, BLOCK], F32, tag="comp", name="comp")
-            nc.scalar.activation(out=comp[:], in_=st["acc", b, n][:], func=ACT.Silu,
-                                 bias=percol[:, 1, n:n + 1], scale=1.0)
-            st["comp", b, n] = comp
-
-        def gatemul(b, n):
-            res = acts.tile([P, BLOCK], F32, tag="res", name="res")
-            nc.vector.scalar_tensor_tensor(out=res[:], in0=st["acc", b, NQ + n][:], scalar=percol[:, 0, n:n + 1],
-                                           in1=st["comp", b, n][:], op0=ALU.is_gt, op1=ALU.mult)
-            st["res", b, n] = res
-
-        def to(b, n):
-            bank = psum.tile([P, SUB, F], F32, tag="bank", name="back")
+        def mx_b(b, n, kind):
+            codes, scales = st["q", b]
+            s = w_slot[n, kind]
+            acc = psum.tile([P, SUB, F], F32, tag="bank", name="acc")
             for j in range(SUB):
-                nc.tensor.transpose(bank[:, j, :], st["res", b, n][:, j * P:(j + 1) * P], ident[:])
-            st["back", b, n] = bank
+                nc.tensor.matmul_mx(out=acc[:, j, :], lhsT=codes[:, j * P:(j + 1) * P].bitcast(FP8X4),
+                                    lhsT_scale=scales[:, j * P:(j + 1) * P],
+                                    rhs=w_codes[:, s * F:(s + 1) * F].bitcast(FP8X4),
+                                    rhs_scale=w_scales[:, s * F:(s + 1) * F], start=True, stop=True)
+            st["acc", b, n, kind] = acc
 
-        def oc(b, n, engine_copy):
-            o_t = outs.tile([P, SUB * F], F32, tag="o", name="o")
-            engine_copy(out=o_t[:], in_=st["back", b, n][:].rearrange("p j f -> p (j f)"))
+        def store(b, n, o_t):
             nc.sync.dma_start(out=out_blocks[b, :, n, :], in_=o_t[:])
 
-        def ok(b):
-            return 0 <= b < NB
+        def silu_a(b):
+            comp = acts.tile([P, BLOCK], F32, tag="comp", name="comp")
+            nc.scalar.activation(out=comp[:], in_=st["acc", b, 0, 0][:], func=ACT.Silu, bias=bias0, scale=1.0)
+            st["comp", b] = comp
 
-        for p in range(-2, NB + 1):
-            if ok(p + 1):
-                ic(p + 1, 0)
-                ic(p + 1, 1)
-                quant(p + 1)
-            if ok(p):
-                for i in (0, 1, NQ, NQ + 1, 2, NQ + 2):
-                    mx(p, i)
-                for n in range(NQ):
-                    silu(p, n)
-                for n in range(NQ):
-                    gatemul(p, n)
-            if ok(p - 1):
-                to(p - 1, 2)
-            if ok(p + 2):
-                ti(p + 2, 0)
-            if ok(p):
-                to(p, 0)
-            if ok(p + 2):
-                ti(p + 2, 1)
-            if ok(p):
-                to(p, 1)
-            if ok(p - 1):
-                oc(p - 1, 2, nc.scalar.copy)
-            if ok(p):
-                oc(p, 0, nc.vector.tensor_copy)
-                oc(p, 1, nc.vector.tensor_copy)
+        def gate_a(b):
+            res = acts.tile([P, BLOCK], F32, tag="res", name="res")
+            nc.vector.scalar_tensor_tensor(out=res[:], in0=st["acc", b, 0, 1][:], scalar=thr0[:, 0:1],
+                                           in1=st["comp", b][:], op0=ALU.is_gt, op1=ALU.mult)
+            st["res", b] = res
+
+        def to(b):
+            bank = psum.tile([P, SUB, F], F32, tag="bank", name="back")
+            for j in range(SUB):
+                nc.tensor.transpose(bank[:, j, :], st["res", b][:, j * P:(j + 1) * P], ident[:])
+            st["back", b] = bank
+
+        def oc(b):
+            o_t = outs.tile([P, SUB * F], F32, tag="o", name="o")
+            nc.scalar.copy(out=o_t[:], in_=st["back", b][:].rearrange("p j f -> p (j f)"))
+            store(b, 0, o_t)
+
+        def bias_b(b, n):
+            t_t = acts.tile([P, SUB, F], F32, tag="t", name="t")
+            vec = cb[:, (n - 1) * F:n * F].unsqueeze(1).to_broadcast([P, SUB, F])
+            nc.vector.tensor_tensor(out=t_t[:], in0=st["acc", b, n, 0][:], in1=vec, op=ALU.add)
+            st["t", b, n] = t_t
+
+        def mask_b(b, n):
+            k_t = acts.tile([P, SUB, F], F32, tag="k", name="k")
+            vec = ca[:, n * F:(n + 1) * F].unsqueeze(1).to_broadcast([P, SUB, F])
+            nc.vector.scalar_tensor_tensor(out=k_t[:], in0=st["acc", b, n, 1][:], scalar=cs[:, n:n + 1],
+                                           in1=vec, op0=ALU.mult, op1=ALU.is_gt)
+            st["k", b, n] = k_t
+
+        def silu_b(b, n):
+            c_t = acts.tile([P, SUB * F], F32, tag="c", name="c")
+            nc.scalar.activation(out=c_t[:], in_=st["t", b, n][:].rearrange("p j f -> p (j f)"), func=ACT.Silu)
+            st["c", b, n] = c_t
+
+        def mul_b(b, n, engine):
+            o_t = outs.tile([P, SUB * F], F32, tag="o", name="o")
+            engine.tensor_tensor(out=o_t[:], in0=st["c", b, n][:],
+                                 in1=st["k", b, n][:].rearrange("p j f -> p (j f)"), op=ALU.mult)
+            store(b, n, o_t)
+
+        ti(0, 0)
+        ti(0, 1)
+        ic(0, 0)
+        ic(0, 1)
+        wf(1)
+        wf(2)
+        quant(0)
+        wc(1, nc.vector.tensor_copy)
+        wc(2, nc.scalar.copy)
+        wq(1)
+        wq(2)
+        ti(1, 0)
+        ti(1, 1)
+        ic(1, 0)
+        ic(1, 1)
+
+        for p in range(NB + 1):
+            live = p < NB
+            if live:
+                mx_a(p, 0)
+                mx_b(p, 1, 0)
+                mx_a(p, 1)
+                mx_b(p, 1, 1)
+                mx_b(p, 2, 0)
+                mx_b(p, 2, 1)
+                silu_a(p)
+            if p >= 1:
+                silu_b(p - 1, 2)
+                mul_b(p - 1, 2, nc.gpsimd if live else nc.vector)
+            if live:
+                bias_b(p, 1)
+                gate_a(p)
+                if p + 1 < NB:
+                    quant(p + 1)
+                mask_b(p, 1)
+                bias_b(p, 2)
+                mask_b(p, 2)
+                silu_b(p, 1)
+                mul_b(p, 1, nc.gpsimd)
+                if p + 2 < NB:
+                    ti(p + 2, 0)
+                to(p)
+                if p + 2 < NB:
+                    ti(p + 2, 1)
+                    ic(p + 2, 0)
+                oc(p)
+                if p + 2 < NB:
+                    ic(p + 2, 1)

@@ -41,7 +41,7 @@ def tile_moietransformerblock_pa_t_kernel(tc, h_ln, mu_w, mu_b, proto_state, gat
         const = ctx.enter_context(tc.tile_pool(name="const", bufs=1))
         xs = ctx.enter_context(tc.tile_pool(name="xs", bufs=NB))
         work = ctx.enter_context(tc.tile_pool(name="work", bufs=3))
-        acts = ctx.enter_context(tc.tile_pool(name="acts", bufs=4))
+        acts = ctx.enter_context(tc.tile_pool(name="acts", bufs=3))
         outs = ctx.enter_context(tc.tile_pool(name="outs", bufs=8))
         psum = ctx.enter_context(tc.psum_pool(name="psum", bufs=8))
         ctx.enter_context(tc.manual_schedule())
@@ -92,13 +92,6 @@ def tile_moietransformerblock_pa_t_kernel(tc, h_ln, mu_w, mu_b, proto_state, gat
             dst = grouped[:].bitcast(F32).rearrange("p (c u) -> p c u", u=2)
             engine_copy(out=dst[:, half * 2 * P:(half + 1) * 2 * P, :], in_=bank[:].rearrange("p u c -> p c u"))
 
-        first_row = ident_bf[:, 0:1].to_broadcast([P, P])
-        ca_ps = psum.tile([P, 4 * F], F32, tag="bank", name="ca_ps")
-        nc.tensor.matmul(out=ca_ps[:], lhsT=first_row, rhs=row_all[:, 0:4 * F], start=True, stop=True)
-        cb_ps = psum.tile([P, 4 * F], F32, tag="bank", name="cb_ps")
-        nc.tensor.matmul(out=cb_ps[:, 0:2 * F], lhsT=first_row, rhs=row_all[:, 4 * F:6 * F], start=True, stop=True)
-        nc.tensor.matmul(out=cb_ps[:, 2 * F:2 * F + 64], lhsT=row_a[:], rhs=ident_bf[:, 0:64], start=True, stop=True)
-
         w_words = w_raw[:].bitcast(F32)
         w_grouped = const.tile([P, 2 * NQ * F * 4], BF16, align_bytes=64)
         w_codes = const.tile([P, 2 * NQ * F], U32, align_bytes=64)
@@ -116,36 +109,15 @@ def tile_moietransformerblock_pa_t_kernel(tc, h_ln, mu_w, mu_b, proto_state, gat
                                   scales=w_scales[:, t * 256:(t + 1) * 256],
                                   in_=w_grouped[:, t * 1024:(t + 1) * 1024])
 
-        wf(0)
-        wc(0, nc.scalar.copy)
-
-        ca = const.tile([P, 4 * F], F32)
-        nc.vector.tensor_copy(out=ca[:], in_=ca_ps[:])
-        cb = const.tile([P, 2 * F + 64], F32)
-        nc.vector.tensor_copy(out=cb[:], in_=cb_ps[:, 0:2 * F + 64])
-        mag = const.tile([P, NQ, F], F32)
-        nc.vector.tensor_scalar_mul(out=mag[:].rearrange("p n f -> p (n f)"), in0=ca[:, 0:NQ * F], scalar1=-1.0)
-        nc.vector.tensor_max(out=mag[:].rearrange("p n f -> p (n f)"), in0=mag[:].rearrange("p n f -> p (n f)"),
-                             in1=ca[:, 0:NQ * F])
-        cs = const.tile([P, NQ], F32)
-        nc.vector.reduce_max(out=cs[:], in_=mag[:], axis=AX.X)
-        nc.vector.tensor_scalar(out=cs[:], in0=cs[:], scalar1=GATE_EPS, scalar2=1.0 / math.sqrt(D),
-                                op0=ALU.add, op1=ALU.mult)
-        thr0 = const.tile([P, 1], F32)
-        nc.vector.reciprocal(out=thr0[:], in_=cs[:, 0:1])
-        nc.vector.tensor_mul(out=thr0[:], in0=thr0[:], in1=cb[:, 2 * F:2 * F + 1])
-        bias0 = cb[:, 2 * F + 1:2 * F + 2]
-        wq(0)
-
         st = {}
 
         def ti(b, h):
             st["in", b, h] = flip(x_raw[b][:].bitcast(F32), 2 * h)
 
-        def ic(b, h):
+        def ic(b, h, engine_copy):
             if h == 0:
                 st["g", b] = work.tile([P, BLOCK * 4], BF16, tag="g", name="g", align_bytes=64)
-            regroup(nc.scalar.copy, st["g", b], h, st["in", b, h])
+            regroup(engine_copy, st["g", b], h, st["in", b, h])
 
         def quant(b):
             codes = work.tile([P, BLOCK], U32, tag="codes", name="codes", align_bytes=64)
@@ -176,6 +148,49 @@ def tile_moietransformerblock_pa_t_kernel(tc, h_ln, mu_w, mu_b, proto_state, gat
         def store(b, n, o_t):
             nc.sync.dma_start(out=out_blocks[b, :, n, :], in_=o_t[:])
 
+        wf(0)
+        wc(0, nc.vector.tensor_copy)
+        wq(0)
+        ti(0, 0)
+        ti(0, 1)
+        ic(0, 0, nc.scalar.copy)
+        ic(0, 1, nc.vector.tensor_copy)
+        quant(0)
+        wf(1)
+        wf(2)
+        wc(1, nc.scalar.copy)
+        wc(2, nc.scalar.copy)
+        wq(1)
+        wq(2)
+
+        first_row = ident_bf[:, 0:1].to_broadcast([P, P])
+        ca_ps = psum.tile([P, 4 * F], F32, tag="bank", name="ca_ps")
+        nc.tensor.matmul(out=ca_ps[:], lhsT=first_row, rhs=row_all[:, 0:4 * F], start=True, stop=True)
+        cb_ps = psum.tile([P, 4 * F], F32, tag="bank", name="cb_ps")
+        nc.tensor.matmul(out=cb_ps[:, 0:2 * F], lhsT=first_row, rhs=row_all[:, 4 * F:6 * F], start=True, stop=True)
+        nc.tensor.matmul(out=cb_ps[:, 2 * F:2 * F + 64], lhsT=row_a[:], rhs=ident_bf[:, 0:64], start=True, stop=True)
+        ca = const.tile([P, 4 * F], F32)
+        nc.vector.tensor_copy(out=ca[:], in_=ca_ps[:])
+        cb = const.tile([P, 2 * F + 64], F32)
+        nc.vector.tensor_copy(out=cb[:], in_=cb_ps[:, 0:2 * F + 64])
+        mag = const.tile([P, NQ, F], F32)
+        nc.vector.tensor_scalar_mul(out=mag[:].rearrange("p n f -> p (n f)"), in0=ca[:, 0:NQ * F], scalar1=-1.0)
+        nc.vector.tensor_max(out=mag[:].rearrange("p n f -> p (n f)"), in0=mag[:].rearrange("p n f -> p (n f)"),
+                             in1=ca[:, 0:NQ * F])
+        cs = const.tile([P, NQ], F32)
+        nc.vector.reduce_max(out=cs[:], in_=mag[:], axis=AX.X)
+        nc.vector.tensor_scalar(out=cs[:], in0=cs[:], scalar1=GATE_EPS, scalar2=1.0 / math.sqrt(D),
+                                op0=ALU.add, op1=ALU.mult)
+        thr0 = const.tile([P, 1], F32)
+        nc.vector.reciprocal(out=thr0[:], in_=cs[:, 0:1])
+        nc.vector.tensor_mul(out=thr0[:], in0=thr0[:], in1=cb[:, 2 * F:2 * F + 1])
+        bias0 = cb[:, 2 * F + 1:2 * F + 2]
+
+        ti(1, 0)
+        ti(1, 1)
+        ic(1, 0, nc.scalar.copy)
+        ic(1, 1, nc.scalar.copy)
+
         def silu_a(b):
             comp = acts.tile([P, BLOCK], F32, tag="comp", name="comp")
             nc.scalar.activation(out=comp[:], in_=st["acc", b, 0, 0][:], func=ACT.Silu, bias=bias0, scale=1.0)
@@ -199,47 +214,34 @@ def tile_moietransformerblock_pa_t_kernel(tc, h_ln, mu_w, mu_b, proto_state, gat
             store(b, 0, o_t)
 
         def bias_b(b, n):
-            t_t = acts.tile([P, SUB, F], F32, tag="t", name="t")
+            if n == 1:
+                st["t", b] = acts.tile([P, 2, SUB, F], F32, tag="t", name="t")
             vec = cb[:, (n - 1) * F:n * F].unsqueeze(1).to_broadcast([P, SUB, F])
-            nc.vector.tensor_tensor(out=t_t[:], in0=st["acc", b, n, 0][:], in1=vec, op=ALU.add)
-            st["t", b, n] = t_t
+            nc.vector.tensor_tensor(out=st["t", b][:, n - 1, :, :], in0=st["acc", b, n, 0][:], in1=vec, op=ALU.add)
 
         def mask_b(b, n):
-            k_t = acts.tile([P, SUB, F], F32, tag="k", name="k")
+            if n == 1:
+                st["k", b] = acts.tile([P, 2, SUB, F], F32, tag="k", name="k")
             vec = ca[:, n * F:(n + 1) * F].unsqueeze(1).to_broadcast([P, SUB, F])
-            nc.vector.scalar_tensor_tensor(out=k_t[:], in0=st["acc", b, n, 1][:], scalar=cs[:, n:n + 1],
-                                           in1=vec, op0=ALU.mult, op1=ALU.is_gt)
-            st["k", b, n] = k_t
+            nc.vector.scalar_tensor_tensor(out=st["k", b][:, n - 1, :, :], in0=st["acc", b, n, 1][:],
+                                           scalar=cs[:, n:n + 1], in1=vec, op0=ALU.mult, op1=ALU.is_gt)
 
-        def silu_b(b, n):
-            c_t = acts.tile([P, SUB * F], F32, tag="c", name="c")
-            nc.scalar.activation(out=c_t[:], in_=st["t", b, n][:].rearrange("p j f -> p (j f)"), func=ACT.Silu)
-            st["c", b, n] = c_t
+        def silu_b(b):
+            c_t = acts.tile([P, 2, SUB * F], F32, tag="c", name="c")
+            nc.scalar.activation(out=c_t[:].rearrange("p n c -> p (n c)"),
+                                 in_=st["t", b][:].rearrange("p n j f -> p (n j f)"), func=ACT.Silu)
+            st["c", b] = c_t
 
         def mul_b(b, n, engine):
             o_t = outs.tile([P, SUB * F], F32, tag="o", name="o")
-            engine.tensor_tensor(out=o_t[:], in0=st["c", b, n][:],
-                                 in1=st["k", b, n][:].rearrange("p j f -> p (j f)"), op=ALU.mult)
+            engine.tensor_tensor(out=o_t[:], in0=st["c", b][:, n - 1, :],
+                                 in1=st["k", b][:, n - 1, :, :].rearrange("p j f -> p (j f)"), op=ALU.mult)
             store(b, n, o_t)
-
-        ti(0, 0)
-        ti(0, 1)
-        ic(0, 0)
-        ic(0, 1)
-        wf(1)
-        wf(2)
-        quant(0)
-        wc(1, nc.vector.tensor_copy)
-        wc(2, nc.scalar.copy)
-        wq(1)
-        wq(2)
-        ti(1, 0)
-        ti(1, 1)
-        ic(1, 0)
-        ic(1, 1)
 
         for p in range(NB + 1):
             live = p < NB
+            if p + 1 < NB:
+                quant(p + 1)
             if live:
                 mx_a(p, 0)
                 mx_b(p, 1, 0)
@@ -248,25 +250,22 @@ def tile_moietransformerblock_pa_t_kernel(tc, h_ln, mu_w, mu_b, proto_state, gat
                 mx_b(p, 2, 0)
                 mx_b(p, 2, 1)
                 silu_a(p)
-            if p >= 1:
-                silu_b(p - 1, 2)
-                mul_b(p - 1, 2, nc.gpsimd if live else nc.vector)
-            if live:
-                bias_b(p, 1)
                 gate_a(p)
-                if p + 1 < NB:
-                    quant(p + 1)
+                bias_b(p, 1)
                 mask_b(p, 1)
                 bias_b(p, 2)
                 mask_b(p, 2)
-                silu_b(p, 1)
-                mul_b(p, 1, nc.gpsimd)
+            if p >= 1:
+                silu_b(p - 1)
+                mul_b(p - 1, 1, nc.gpsimd if live else nc.vector)
+                mul_b(p - 1, 2, nc.gpsimd if live else nc.vector)
+            if live:
                 if p + 2 < NB:
                     ti(p + 2, 0)
                 to(p)
                 if p + 2 < NB:
                     ti(p + 2, 1)
-                    ic(p + 2, 0)
+                    ic(p + 2, 0, nc.scalar.copy)
                 oc(p)
                 if p + 2 < NB:
-                    ic(p + 2, 1)
+                    ic(p + 2, 1, nc.scalar.copy)

@@ -23,6 +23,7 @@ BLOCK = 512
 SUB = BLOCK // P
 NB = TOKENS // BLOCK
 GATE_EPS = 1e-9
+WARM = 0
 
 FLOPS = 2 * TOKENS * D * 2 * NQ * F
 
@@ -46,14 +47,11 @@ def tile_moietransformerblock_pa_t_kernel(tc, h_ln, mu_w, mu_b, proto_state, gat
         psum = ctx.enter_context(tc.psum_pool(name="psum", bufs=8))
         ctx.enter_context(tc.manual_schedule())
 
+        row_one = const.tile([1, 2 * NQ * F], BF16)
+        nc.scalar.dma_start(out=row_one[:, 0:NQ * F], in_=gate.rearrange("(o n) f -> o (n f)", o=1))
+        nc.scalar.dma_start(out=row_one[:, NQ * F:2 * NQ * F], in_=mu_b.rearrange("(o n) f -> o (n f)", o=1))
         row_all = const.tile([P, 2 * NQ * F], BF16)
-        nc.vector.memset(row_all[:], 0.0)
-        row_a = const.tile([P, F], BF16)
-        nc.vector.memset(row_a[:], 0.0)
-        nc.scalar.dma_start(out=row_all[0:1, 0:NQ * F], in_=gate.rearrange("(o n) f -> o (n f)", o=1))
-        nc.scalar.dma_start(out=row_all[0:1, NQ * F:2 * NQ * F], in_=mu_b.rearrange("(o n) f -> o (n f)", o=1))
-        nc.scalar.dma_start(out=row_a[0:1, :], in_=gate[0:1, :])
-        nc.scalar.dma_start(out=row_a[1:2, :], in_=mu_b[0:1, :])
+        nc.vector.memset(row_all[:].bitcast(mybir.dt.int32), 0)
 
         w_raw = const.tile([P, 2 * NQ * D], BF16)
         x_raw = []
@@ -72,13 +70,21 @@ def tile_moietransformerblock_pa_t_kernel(tc, h_ln, mu_w, mu_b, proto_state, gat
         for b in range(1, NB):
             nc.sync.dma_start(out=x_raw[b][:], in_=h_blocks[b])
 
-        ident = const.tile([P, P], F32)
-        make_identity(nc, ident[:])
         ident_bf = const.tile([P, P], BF16)
         make_identity(nc, ident_bf[:])
+        ident = const.tile([P, P], F32)
+        make_identity(nc, ident[:])
         warm = const.tile([P, 2], F32)
         nc.vector.memset(warm[:], 0.0)
         nc.scalar.activation(out=warm[:, 1:2], in_=warm[:, 0:1], func=ACT.Silu)
+        nc.scalar.copy(out=row_all[0:1, :], in_=row_one[:])
+
+        if WARM:
+            idle = const.tile([P, BLOCK], BF16)
+            nc.vector.memset(idle[:], 0.0)
+            idle_ps = psum.tile([P, BLOCK], F32, tag="bank", name="idle_ps")
+            for i in range(WARM):
+                nc.tensor.matmul(out=idle_ps[:], lhsT=idle[:, 0:P], rhs=idle[:], start=True, stop=True)
 
         def flip(src_words, first):
             bank = psum.tile([P, 2, 2 * P], F32, tag="bank", name="flip")
@@ -91,6 +97,14 @@ def tile_moietransformerblock_pa_t_kernel(tc, h_ln, mu_w, mu_b, proto_state, gat
         def regroup(engine_copy, grouped, half, bank):
             dst = grouped[:].bitcast(F32).rearrange("p (c u) -> p c u", u=2)
             engine_copy(out=dst[:, half * 2 * P:(half + 1) * 2 * P, :], in_=bank[:].rearrange("p u c -> p c u"))
+
+        first_row = ident_bf[:, 0:1].to_broadcast([P, P])
+        ca = const.tile([P, 4 * F], F32)
+        cb = const.tile([P, 3 * F], F32)
+        cs = const.tile([P, NQ], F32)
+        low = const.tile([P, NQ], F32)
+        thr0 = const.tile([P, 1], F32)
+        bias0 = cb[:, 2 * F + 64:2 * F + 65]
 
         w_words = w_raw[:].bitcast(F32)
         w_grouped = const.tile([P, 2 * NQ * F * 4], BF16, align_bytes=64)
@@ -145,51 +159,8 @@ def tile_moietransformerblock_pa_t_kernel(tc, h_ln, mu_w, mu_b, proto_state, gat
                                     rhs_scale=w_scales[:, s * F:(s + 1) * F], start=True, stop=True)
             st["acc", b, n, kind] = acc
 
-        def store(b, n, o_t):
-            nc.sync.dma_start(out=out_blocks[b, :, n, :], in_=o_t[:])
-
-        wf(0)
-        wc(0, nc.vector.tensor_copy)
-        wq(0)
-        ti(0, 0)
-        ti(0, 1)
-        ic(0, 0, nc.scalar.copy)
-        ic(0, 1, nc.vector.tensor_copy)
-        quant(0)
-        wf(1)
-        wf(2)
-        wc(1, nc.scalar.copy)
-        wc(2, nc.scalar.copy)
-        wq(1)
-        wq(2)
-
-        first_row = ident_bf[:, 0:1].to_broadcast([P, P])
-        ca_ps = psum.tile([P, 4 * F], F32, tag="bank", name="ca_ps")
-        nc.tensor.matmul(out=ca_ps[:], lhsT=first_row, rhs=row_all[:, 0:4 * F], start=True, stop=True)
-        cb_ps = psum.tile([P, 4 * F], F32, tag="bank", name="cb_ps")
-        nc.tensor.matmul(out=cb_ps[:, 0:2 * F], lhsT=first_row, rhs=row_all[:, 4 * F:6 * F], start=True, stop=True)
-        nc.tensor.matmul(out=cb_ps[:, 2 * F:2 * F + 64], lhsT=row_a[:], rhs=ident_bf[:, 0:64], start=True, stop=True)
-        ca = const.tile([P, 4 * F], F32)
-        nc.vector.tensor_copy(out=ca[:], in_=ca_ps[:])
-        cb = const.tile([P, 2 * F + 64], F32)
-        nc.vector.tensor_copy(out=cb[:], in_=cb_ps[:, 0:2 * F + 64])
-        mag = const.tile([P, NQ, F], F32)
-        nc.vector.tensor_scalar_mul(out=mag[:].rearrange("p n f -> p (n f)"), in0=ca[:, 0:NQ * F], scalar1=-1.0)
-        nc.vector.tensor_max(out=mag[:].rearrange("p n f -> p (n f)"), in0=mag[:].rearrange("p n f -> p (n f)"),
-                             in1=ca[:, 0:NQ * F])
-        cs = const.tile([P, NQ], F32)
-        nc.vector.reduce_max(out=cs[:], in_=mag[:], axis=AX.X)
-        nc.vector.tensor_scalar(out=cs[:], in0=cs[:], scalar1=GATE_EPS, scalar2=1.0 / math.sqrt(D),
-                                op0=ALU.add, op1=ALU.mult)
-        thr0 = const.tile([P, 1], F32)
-        nc.vector.reciprocal(out=thr0[:], in_=cs[:, 0:1])
-        nc.vector.tensor_mul(out=thr0[:], in0=thr0[:], in1=cb[:, 2 * F:2 * F + 1])
-        bias0 = cb[:, 2 * F + 1:2 * F + 2]
-
-        ti(1, 0)
-        ti(1, 1)
-        ic(1, 0, nc.scalar.copy)
-        ic(1, 1, nc.scalar.copy)
+        def store(b, n, src):
+            nc.sync.dma_start(out=out_blocks[b, :, n, :], in_=src)
 
         def silu_a(b):
             comp = acts.tile([P, BLOCK], F32, tag="comp", name="comp")
@@ -211,37 +182,72 @@ def tile_moietransformerblock_pa_t_kernel(tc, h_ln, mu_w, mu_b, proto_state, gat
         def oc(b):
             o_t = outs.tile([P, SUB * F], F32, tag="o", name="o")
             nc.scalar.copy(out=o_t[:], in_=st["back", b][:].rearrange("p j f -> p (j f)"))
-            store(b, 0, o_t)
+            store(b, 0, o_t[:])
 
         def bias_b(b, n):
-            if n == 1:
-                st["t", b] = acts.tile([P, 2, SUB, F], F32, tag="t", name="t")
+            t_t = acts.tile([P, SUB, F], F32, tag="t", name="t", bufs=4)
             vec = cb[:, (n - 1) * F:n * F].unsqueeze(1).to_broadcast([P, SUB, F])
-            nc.vector.tensor_tensor(out=st["t", b][:, n - 1, :, :], in0=st["acc", b, n, 0][:], in1=vec, op=ALU.add)
+            nc.vector.tensor_tensor(out=t_t[:], in0=st["acc", b, n, 0][:], in1=vec, op=ALU.add)
+            st["t", b, n] = t_t
 
         def mask_b(b, n):
-            if n == 1:
-                st["k", b] = acts.tile([P, 2, SUB, F], F32, tag="k", name="k")
+            k_t = acts.tile([P, SUB, F], F32, tag="k", name="k", bufs=6)
             vec = ca[:, n * F:(n + 1) * F].unsqueeze(1).to_broadcast([P, SUB, F])
-            nc.vector.scalar_tensor_tensor(out=st["k", b][:, n - 1, :, :], in0=st["acc", b, n, 1][:],
-                                           scalar=cs[:, n:n + 1], in1=vec, op0=ALU.mult, op1=ALU.is_gt)
+            nc.vector.scalar_tensor_tensor(out=k_t[:], in0=st["acc", b, n, 1][:], scalar=cs[:, n:n + 1],
+                                           in1=vec, op0=ALU.mult, op1=ALU.is_gt)
+            st["k", b, n] = k_t
 
-        def silu_b(b):
-            c_t = acts.tile([P, 2, SUB * F], F32, tag="c", name="c")
-            nc.scalar.activation(out=c_t[:].rearrange("p n c -> p (n c)"),
-                                 in_=st["t", b][:].rearrange("p n j f -> p (n j f)"), func=ACT.Silu)
-            st["c", b] = c_t
+        def silu_b(b, n):
+            c_t = acts.tile([P, SUB * F], F32, tag="c", name="c", bufs=4)
+            nc.scalar.activation(out=c_t[:], in_=st["t", b, n][:].rearrange("p j f -> p (j f)"), func=ACT.Silu)
+            st["c", b, n] = c_t
 
         def mul_b(b, n, engine):
             o_t = outs.tile([P, SUB * F], F32, tag="o", name="o")
-            engine.tensor_tensor(out=o_t[:], in0=st["c", b][:, n - 1, :],
-                                 in1=st["k", b][:, n - 1, :, :].rearrange("p j f -> p (j f)"), op=ALU.mult)
-            store(b, n, o_t)
+            engine.tensor_tensor(out=o_t[:], in0=st["c", b, n][:],
+                                 in1=st["k", b, n][:].rearrange("p j f -> p (j f)"), op=ALU.mult)
+            store(b, n, o_t[:])
+
+        wf(0)
+        wc(0, nc.scalar.copy)
+        ca_ps = psum.tile([P, 4 * F], F32, tag="bank", name="ca_ps")
+        cb_ps = psum.tile([P, 4 * F], F32, tag="bank", name="cb_ps")
+        nc.tensor.matmul(out=ca_ps[:], lhsT=first_row, rhs=row_all[:, 0:4 * F], start=True, stop=True)
+        nc.tensor.matmul(out=cb_ps[:, 0:2 * F], lhsT=first_row, rhs=row_all[:, 4 * F:6 * F], start=True, stop=True)
+        nc.tensor.matmul(out=cb_ps[:, 2 * F:2 * F + 64], lhsT=row_all[:, 0:F], rhs=ident_bf[:, 0:64],
+                         start=True, stop=True)
+        nc.tensor.matmul(out=cb_ps[:, 2 * F + 64:3 * F], lhsT=row_all[:, NQ * F:(NQ + 1) * F], rhs=ident_bf[:, 0:64],
+                         start=True, stop=True)
+        gates_ps = ca_ps[:, 0:NQ * F].rearrange("p (n f) -> p n f", n=NQ)
+        nc.vector.tensor_reduce(out=low[:], in_=gates_ps, axis=AX.X, op=ALU.min)
+        nc.vector.reduce_max(out=cs[:], in_=gates_ps, axis=AX.X)
+        nc.vector.tensor_scalar_mul(out=low[:], in0=low[:], scalar1=-1.0)
+        nc.vector.tensor_max(out=cs[:], in0=cs[:], in1=low[:])
+        nc.vector.tensor_scalar(out=cs[:], in0=cs[:], scalar1=GATE_EPS, scalar2=1.0 / math.sqrt(D),
+                                op0=ALU.add, op1=ALU.mult)
+        nc.vector.reciprocal(out=thr0[:], in_=cs[:, 0:1])
+        nc.vector.tensor_copy(out=cb[:], in_=cb_ps[:, 0:3 * F])
+        nc.vector.tensor_mul(out=thr0[:], in0=thr0[:], in1=cb[:, 2 * F:2 * F + 1])
+        wq(0)
+        nc.vector.tensor_copy(out=ca[:], in_=ca_ps[:])
+        ti(0, 0)
+        ti(0, 1)
+        ic(0, 0, nc.scalar.copy)
+        ic(0, 1, nc.scalar.copy)
+        quant(0)
+        wf(1)
+        wf(2)
+        wc(1, nc.scalar.copy)
+        wc(2, nc.scalar.copy)
+        wq(1)
+        wq(2)
+        ti(1, 0)
+        ti(1, 1)
+        ic(1, 0, nc.scalar.copy)
+        ic(1, 1, nc.scalar.copy)
 
         for p in range(NB + 1):
             live = p < NB
-            if p + 1 < NB:
-                quant(p + 1)
             if live:
                 mx_a(p, 0)
                 mx_b(p, 1, 0)
@@ -250,16 +256,19 @@ def tile_moietransformerblock_pa_t_kernel(tc, h_ln, mu_w, mu_b, proto_state, gat
                 mx_b(p, 2, 0)
                 mx_b(p, 2, 1)
                 silu_a(p)
-                gate_a(p)
+            if p >= 1:
+                silu_b(p - 1, 2)
+                mul_b(p - 1, 2, nc.gpsimd if live else nc.vector)
+            if live:
                 bias_b(p, 1)
+                gate_a(p)
+                if p + 1 < NB:
+                    quant(p + 1)
                 mask_b(p, 1)
                 bias_b(p, 2)
                 mask_b(p, 2)
-            if p >= 1:
-                silu_b(p - 1)
-                mul_b(p - 1, 1, nc.gpsimd if live else nc.vector)
-                mul_b(p - 1, 2, nc.gpsimd if live else nc.vector)
-            if live:
+                silu_b(p, 1)
+                mul_b(p, 1, nc.gpsimd)
                 if p + 2 < NB:
                     ti(p + 2, 0)
                 to(p)

@@ -248,33 +248,33 @@ def tile_moietransformerblock_pa_t_kernel(tc, h_ln, mu_w, mu_b, proto_state, gat
 
         for p in range(NB + 1):
             live = p < NB
+            ahead = p + 2 < NB
             if live:
-                mx_a(p, 0)
                 mx_b(p, 1, 0)
+                mx_a(p, 0)
                 mx_a(p, 1)
-                mx_b(p, 1, 1)
-                mx_b(p, 2, 0)
-                mx_b(p, 2, 1)
+                bias_b(p, 1)
+                if p + 1 < NB:
+                    quant(p + 1)
                 silu_a(p)
+                gate_a(p)
             if p >= 1:
                 silu_b(p - 1, 2)
                 mul_b(p - 1, 2, nc.gpsimd if live else nc.vector)
             if live:
-                bias_b(p, 1)
-                gate_a(p)
-                if p + 1 < NB:
-                    quant(p + 1)
+                if ahead:
+                    ti(p + 2, 0)
+                    ic(p + 2, 0, nc.scalar.copy)
+                mx_b(p, 1, 1)
+                mx_b(p, 2, 0)
+                mx_b(p, 2, 1)
                 mask_b(p, 1)
                 bias_b(p, 2)
                 mask_b(p, 2)
                 silu_b(p, 1)
                 mul_b(p, 1, nc.gpsimd)
-                if p + 2 < NB:
-                    ti(p + 2, 0)
-                to(p)
-                if p + 2 < NB:
+                if ahead:
                     ti(p + 2, 1)
-                    ic(p + 2, 0, nc.scalar.copy)
-                oc(p)
-                if p + 2 < NB:
                     ic(p + 2, 1, nc.scalar.copy)
+                to(p)
+                oc(p)

@@ -23,7 +23,7 @@ BLOCK = 512
 SUB = BLOCK // P
 NB = TOKENS // BLOCK
 GATE_EPS = 1e-9
-WARM = 0
+WARM = (5, 2)
 
 FLOPS = 2 * TOKENS * D * 2 * NQ * F
 
@@ -79,12 +79,15 @@ def tile_moietransformerblock_pa_t_kernel(tc, h_ln, mu_w, mu_b, proto_state, gat
         nc.scalar.activation(out=warm[:, 1:2], in_=warm[:, 0:1], func=ACT.Silu)
         nc.scalar.copy(out=row_all[0:1, :], in_=row_one[:])
 
-        if WARM:
-            idle = const.tile([P, BLOCK], BF16)
-            nc.vector.memset(idle[:], 0.0)
+        idle = const.tile([P, BLOCK], BF16)
+        nc.vector.memset(idle[:].bitcast(mybir.dt.int32), 0)
+
+        def keep_busy(count):
             idle_ps = psum.tile([P, BLOCK], F32, tag="bank", name="idle_ps")
-            for i in range(WARM):
+            for i in range(count):
                 nc.tensor.matmul(out=idle_ps[:], lhsT=idle[:, 0:P], rhs=idle[:], start=True, stop=True)
+
+        keep_busy(WARM[0])
 
         def flip(src_words, first):
             bank = psum.tile([P, 2, 2 * P], F32, tag="bank", name="flip")
@@ -241,6 +244,7 @@ def tile_moietransformerblock_pa_t_kernel(tc, h_ln, mu_w, mu_b, proto_state, gat
         wc(2, nc.scalar.copy)
         wq(1)
         wq(2)
+        keep_busy(WARM[1])
         ti(1, 0)
         ti(1, 1)
         ic(1, 0, nc.scalar.copy)

@@ -23,7 +23,7 @@ BLOCK = 512
 SUB = BLOCK // P
 NB = TOKENS // BLOCK
 GATE_EPS = 1e-9
-WARM = (5, 2)
+WARM = 0
 
 FLOPS = 2 * TOKENS * D * 2 * NQ * F
 
@@ -79,15 +79,12 @@ def tile_moietransformerblock_pa_t_kernel(tc, h_ln, mu_w, mu_b, proto_state, gat
         nc.scalar.activation(out=warm[:, 1:2], in_=warm[:, 0:1], func=ACT.Silu)
         nc.scalar.copy(out=row_all[0:1, :], in_=row_one[:])
 
-        idle = const.tile([P, BLOCK], BF16)
-        nc.vector.memset(idle[:].bitcast(mybir.dt.int32), 0)
-
-        def keep_busy(count):
+        if WARM:
+            idle = const.tile([P, BLOCK], BF16)
+            nc.vector.memset(idle[:], 0.0)
             idle_ps = psum.tile([P, BLOCK], F32, tag="bank", name="idle_ps")
-            for i in range(count):
+            for i in range(WARM):
                 nc.tensor.matmul(out=idle_ps[:], lhsT=idle[:, 0:P], rhs=idle[:], start=True, stop=True)
-
-        keep_busy(WARM[0])
 
         def flip(src_words, first):
             bank = psum.tile([P, 2, 2 * P], F32, tag="bank", name="flip")
@@ -205,10 +202,13 @@ def tile_moietransformerblock_pa_t_kernel(tc, h_ln, mu_w, mu_b, proto_state, gat
             nc.scalar.activation(out=c_t[:], in_=st["t", b, n][:].rearrange("p j f -> p (j f)"), func=ACT.Silu)
             st["c", b, n] = c_t
 
-        def mul_b(b, n, engine):
+        def mul_b(b, n, engine, pieces):
             o_t = outs.tile([P, SUB * F], F32, tag="o", name="o")
-            engine.tensor_tensor(out=o_t[:], in0=st["c", b, n][:],
-                                 in1=st["k", b, n][:].rearrange("p j f -> p (j f)"), op=ALU.mult)
+            mask = st["k", b, n][:].rearrange("p j f -> p (j f)")
+            step = SUB * F // pieces
+            for i in range(pieces):
+                cols = slice(i * step, (i + 1) * step)
+                engine.tensor_tensor(out=o_t[:, cols], in0=st["c", b, n][:, cols], in1=mask[:, cols], op=ALU.mult)
             store(b, n, o_t[:])
 
         wf(0)
@@ -244,7 +244,6 @@ def tile_moietransformerblock_pa_t_kernel(tc, h_ln, mu_w, mu_b, proto_state, gat
         wc(2, nc.scalar.copy)
         wq(1)
         wq(2)
-        keep_busy(WARM[1])
         ti(1, 0)
         ti(1, 1)
         ic(1, 0, nc.scalar.copy)
@@ -264,7 +263,7 @@ def tile_moietransformerblock_pa_t_kernel(tc, h_ln, mu_w, mu_b, proto_state, gat
                 gate_a(p)
             if p >= 1:
                 silu_b(p - 1, 2)
-                mul_b(p - 1, 2, nc.gpsimd if live else nc.vector)
+                mul_b(p - 1, 2, nc.gpsimd if live else nc.vector, 2 if live else 1)
             if live:
                 if ahead:
                     ti(p + 2, 0)
@@ -276,7 +275,7 @@ def tile_moietransformerblock_pa_t_kernel(tc, h_ln, mu_w, mu_b, proto_state, gat
                 bias_b(p, 2)
                 mask_b(p, 2)
                 silu_b(p, 1)
-                mul_b(p, 1, nc.gpsimd)
+                mul_b(p, 1, nc.gpsimd, 2)
                 if ahead:
                     ti(p + 2, 1)
                     ic(p + 2, 1, nc.scalar.copy)

from contextlib import ExitStack
import math

import concourse.mybir as mybir
from concourse.masks import make_identity

F32 = mybir.dt.float32
BF16 = mybir.dt.bfloat16
U32 = mybir.dt.uint32
U8 = mybir.dt.uint8
FP8X4 = mybir.dt.float8_e4m3fn_x4
ACT = mybir.ActivationFunctionType
ALU = mybir.AluOpType
AX = mybir.AxisListType

P = 128
TOKENS = 8192
D = 512
WORDS = D // 2
F = 128
NQ = 3
BLOCK = 512
SUB = BLOCK // P
NB = TOKENS // BLOCK
GATE_EPS = 1e-9
WARM = 0

FLOPS = 2 * TOKENS * D * 2 * NQ * F

W_ORDER = ((0, 0), (1, 0), (0, 1), (1, 1), (2, 0), (2, 1))


def tile_moietransformerblock_pa_t_kernel(tc, h_ln, mu_w, mu_b, proto_state, gate, out):
    nc = tc.nc
    h_blocks = h_ln.rearrange("a s k -> (a s) k").rearrange("(b p j) k -> b p (j k)", p=P, j=SUB)
    out_blocks = out.rearrange("n a s f -> n (a s) f").rearrange("n (b p j) f -> b p n (j f)", p=P, j=SUB)
    w_slot = {}
    for slot, key in enumerate(W_ORDER):
        w_slot[key] = slot

    with ExitStack() as ctx:
        const = ctx.enter_context(tc.tile_pool(name="const", bufs=1))
        xs = ctx.enter_context(tc.tile_pool(name="xs", bufs=NB))
        work = ctx.enter_context(tc.tile_pool(name="work", bufs=3))
        acts = ctx.enter_context(tc.tile_pool(name="acts", bufs=3))
        outs = ctx.enter_context(tc.tile_pool(name="outs", bufs=8))
        psum = ctx.enter_context(tc.psum_pool(name="psum", bufs=8))
        ctx.enter_context(tc.manual_schedule())

        row_one = const.tile([1, 2 * NQ * F], BF16)
        nc.scalar.dma_start(out=row_one[:, 0:NQ * F], in_=gate.rearrange("(o n) f -> o (n f)", o=1))
        nc.scalar.dma_start(out=row_one[:, NQ * F:2 * NQ * F], in_=mu_b.rearrange("(o n) f -> o (n f)", o=1))
        row_all = const.tile([P, 2 * NQ * F], BF16)
        nc.vector.memset(row_all[:].bitcast(mybir.dt.int32), 0)

        w_raw = const.tile([P, 2 * NQ * D], BF16)
        x_raw = []
        for b in range(NB):
            x_raw.append(xs.tile([P, SUB * D], BF16, tag="x", name="x%d" % b))

        def load_w(src, lo, hi, slot):
            nc.sync.dma_start(out=w_raw[:, slot * D:(slot + hi - lo) * D].rearrange("f (n k) -> f n k", k=D),
                              in_=src[lo:hi].rearrange("n f k -> f n k"))

        load_w(mu_w, 0, 2, 0)
        nc.sync.dma_start(out=x_raw[0][:], in_=h_blocks[0])
        load_w(proto_state, 0, 2, 2)
        load_w(mu_w, 2, 3, 4)
        load_w(proto_state, 2, 3, 5)
        for b in range(1, NB):
            nc.sync.dma_start(out=x_raw[b][:], in_=h_blocks[b])

        ident_bf = const.tile([P, P], BF16)
        make_identity(nc, ident_bf[:])
        ident = const.tile([P, P], F32)
        make_identity(nc, ident[:])
        warm = const.tile([P, 2], F32)
        nc.vector.memset(warm[:], 0.0)
        nc.scalar.activation(out=warm[:, 1:2], in_=warm[:, 0:1], func=ACT.Silu)
        nc.scalar.copy(out=row_all[0:1, :], in_=row_one[:])

        if WARM:
            idle = const.tile([P, BLOCK], BF16)
            nc.vector.memset(idle[:], 0.0)
            idle_ps = psum.tile([P, BLOCK], F32, tag="bank", name="idle_ps")
            for i in range(WARM):
                nc.tensor.matmul(out=idle_ps[:], lhsT=idle[:, 0:P], rhs=idle[:], start=True, stop=True)

        def flip(src_words, first):
            bank = psum.tile([P, 2, 2 * P], F32, tag="bank", name="flip")
            for r in range(2):
                for u in range(2):
                    lo = (first + r) * WORDS + u * P
                    nc.tensor.transpose(bank[:, u, r * P:(r + 1) * P], src_words[:, lo:lo + P], ident[:])
            return bank

        def regroup(engine_copy, grouped, half, bank):
            dst = grouped[:].bitcast(F32).rearrange("p (c u) -> p c u", u=2)
            engine_copy(out=dst[:, half * 2 * P:(half + 1) * 2 * P, :], in_=bank[:].rearrange("p u c -> p c u"))

        first_row = ident_bf[:, 0:1].to_broadcast([P, P])
        ca = const.tile([P, 4 * F], F32)
        cb = const.tile([P, 3 * F], F32)
        cs = const.tile([P, NQ], F32)
        low = const.tile([P, NQ], F32)
        thr0 = const.tile([P, 1], F32)
        bias0 = cb[:, 2 * F + 64:2 * F + 65]

        w_words = w_raw[:].bitcast(F32)
        w_grouped = const.tile([P, 2 * NQ * F * 4], BF16, align_bytes=64)
        w_codes = const.tile([P, 2 * NQ * F], U32, align_bytes=64)
        w_scales = const.tile([P, 2 * NQ * F], U8, align_bytes=64)
        w_banks = {}

        def wf(t):
            w_banks[t] = flip(w_words, 2 * t)

        def wc(t, engine_copy):
            regroup(engine_copy, w_grouped, t, w_banks[t])

        def wq(t):
            nc.vector.quantize_mx(out=w_codes[:, t * 256:(t + 1) * 256].bitcast(FP8X4),
                                  scales=w_scales[:, t * 256:(t + 1) * 256],
                                  in_=w_grouped[:, t * 1024:(t + 1) * 1024])

        st = {}

        def ti(b, h):
            st["in", b, h] = flip(x_raw[b][:].bitcast(F32), 2 * h)

        def ic(b, h, engine_copy):
            if h == 0:
                st["g", b] = work.tile([P, BLOCK * 4], BF16, tag="g", name="g", align_bytes=64)
            regroup(engine_copy, st["g", b], h, st["in", b, h])

        def quant(b):
            codes = work.tile([P, BLOCK], U32, tag="codes", name="codes", align_bytes=64)
            scales = work.tile([P, BLOCK], U8, tag="scales", name="scales", align_bytes=64)
            nc.vector.quantize_mx(out=codes[:].bitcast(FP8X4), scales=scales[:], in_=st["g", b][:])
            st["q", b] = (codes, scales)

        def mx_a(b, kind):
            codes, scales = st["q", b]
            s = w_slot[0, kind]
            acc = psum.tile([P, BLOCK], F32, tag="bank", name="acc")
            nc.tensor.matmul_mx(out=acc[:], lhsT=w_codes[:, s * F:(s + 1) * F].bitcast(FP8X4),
                                lhsT_scale=w_scales[:, s * F:(s + 1) * F],
                                rhs=codes[:].bitcast(FP8X4), rhs_scale=scales[:], start=True, stop=True)
            st["acc", b, 0, kind] = acc

        def mx_b(b, n, kind):
            codes, scales = st["q", b]
            s = w_slot[n, kind]
            acc = psum.tile([P, SUB, F], F32, tag="bank", name="acc")
            for j in range(SUB):
                nc.tensor.matmul_mx(out=acc[:, j, :], lhsT=codes[:, j * P:(j + 1) * P].bitcast(FP8X4),
                                    lhsT_scale=scales[:, j * P:(j + 1) * P],
                                    rhs=w_codes[:, s * F:(s + 1) * F].bitcast(FP8X4),
                                    rhs_scale=w_scales[:, s * F:(s + 1) * F], start=True, stop=True)
            st["acc", b, n, kind] = acc

        def store(b, n, src):
            nc.sync.dma_start(out=out_blocks[b, :, n, :], in_=src)

        def silu_a(b):
            comp = acts.tile([P, BLOCK], F32, tag="comp", name="comp")
            nc.scalar.activation(out=comp[:], in_=st["acc", b, 0, 0][:], func=ACT.Silu, bias=bias0, scale=1.0)
            st["comp", b] = comp

        def gate_a(b):
            res = acts.tile([P, BLOCK], F32, tag="res", name="res")
            nc.vector.scalar_tensor_tensor(out=res[:], in0=st["acc", b, 0, 1][:], scalar=thr0[:, 0:1],
                                           in1=st["comp", b][:], op0=ALU.is_gt, op1=ALU.mult)
            st["res", b] = res

        def to(b):
            bank = psum.tile([P, SUB, F], F32, tag="bank", name="back")
            for j in range(SUB):
                nc.tensor.transpose(bank[:, j, :], st["res", b][:, j * P:(j + 1) * P], ident[:])
            st["back", b] = bank

        def oc(b):
            o_t = outs.tile([P, SUB * F], F32, tag="o", name="o")
            nc.scalar.copy(out=o_t[:], in_=st["back", b][:].rearrange("p j f -> p (j f)"))
            store(b, 0, o_t[:])

        def bias_b(b, n):
            t_t = acts.tile([P, SUB, F], F32, tag="t", name="t", bufs=4)
            vec = cb[:, (n - 1) * F:n * F].unsqueeze(1).to_broadcast([P, SUB, F])
            nc.vector.tensor_tensor(out=t_t[:], in0=st["acc", b, n, 0][:], in1=vec, op=ALU.add)
            st["t", b, n] = t_t

        def mask_b(b, n):
            k_t = acts.tile([P, SUB, F], F32, tag="k", name="k", bufs=6)
            vec = ca[:, n * F:(n + 1) * F].unsqueeze(1).to_broadcast([P, SUB, F])
            nc.vector.scalar_tensor_tensor(out=k_t[:], in0=st["acc", b, n, 1][:], scalar=cs[:, n:n + 1],
                                           in1=vec, op0=ALU.mult, op1=ALU.is_gt)
            st["k", b, n] = k_t

        def silu_b(b, n):
            c_t = acts.tile([P, SUB * F], F32, tag="c", name="c", bufs=4)
            nc.scalar.activation(out=c_t[:], in_=st["t", b, n][:].rearrange("p j f -> p (j f)"), func=ACT.Silu)
            st["c", b, n] = c_t

        def mul_b(b, n, engine, pieces):
            o_t = outs.tile([P, SUB * F], F32, tag="o", name="o")
            mask = st["k", b, n][:].rearrange("p j f -> p (j f)")
            step = SUB * F // pieces
            for i in range(pieces):
                cols = slice(i * step, (i + 1) * step)
                engine.tensor_tensor(out=o_t[:, cols], in0=st["c", b, n][:, cols], in1=mask[:, cols], op=ALU.mult)
            store(b, n, o_t[:])

        wf(0)
        wc(0, nc.scalar.copy)
        ca_ps = psum.tile([P, 4 * F], F32, tag="bank", name="ca_ps")
        cb_ps = psum.tile([P, 4 * F], F32, tag="bank", name="cb_ps")
        nc.tensor.matmul(out=ca_ps[:], lhsT=first_row, rhs=row_all[:, 0:4 * F], start=True, stop=True)
        nc.tensor.matmul(out=cb_ps[:, 0:2 * F], lhsT=first_row, rhs=row_all[:, 4 * F:6 * F], start=True, stop=True)
        nc.tensor.matmul(out=cb_ps[:, 2 * F:2 * F + 64], lhsT=row_all[:, 0:F], rhs=ident_bf[:, 0:64],
                         start=True, stop=True)
        nc.tensor.matmul(out=cb_ps[:, 2 * F + 64:3 * F], lhsT=row_all[:, NQ * F:(NQ + 1) * F], rhs=ident_bf[:, 0:64],
                         start=True, stop=True)
        gates_ps = ca_ps[:, 0:NQ * F].rearrange("p (n f) -> p n f", n=NQ)
        nc.vector.tensor_reduce(out=low[:], in_=gates_ps, axis=AX.X, op=ALU.min)
        nc.vector.reduce_max(out=cs[:], in_=gates_ps, axis=AX.X)
        nc.vector.tensor_scalar_mul(out=low[:], in0=low[:], scalar1=-1.0)
        nc.vector.tensor_max(out=cs[:], in0=cs[:], in1=low[:])
        nc.vector.tensor_scalar(out=cs[:], in0=cs[:], scalar1=GATE_EPS, scalar2=1.0 / math.sqrt(D),
                                op0=ALU.add, op1=ALU.mult)
        nc.vector.reciprocal(out=thr0[:], in_=cs[:, 0:1])
        nc.vector.tensor_copy(out=cb[:], in_=cb_ps[:, 0:3 * F])
        nc.vector.tensor_mul(out=thr0[:], in0=thr0[:], in1=cb[:, 2 * F:2 * F + 1])
        wq(0)
        nc.vector.tensor_copy(out=ca[:], in_=ca_ps[:])
        ti(0, 0)
        ti(0, 1)
        ic(0, 0, nc.scalar.copy)
        ic(0, 1, nc.scalar.copy)
        quant(0)
        wf(1)
        wf(2)
        wc(1, nc.scalar.copy)
        wc(2, nc.scalar.copy)
        wq(1)
        wq(2)
        ti(1, 0)
        ti(1, 1)
        ic(1, 0, nc.scalar.copy)
        ic(1, 1, nc.scalar.copy)

        for p in range(NB + 1):
            live = p < NB
            ahead = p + 2 < NB
            if live:
                mx_b(p, 1, 0)
                mx_a(p, 0)
                mx_a(p, 1)
                bias_b(p, 1)
                if p + 1 < NB:
                    quant(p + 1)
                silu_a(p)
                gate_a(p)
            if p >= 1:
                silu_b(p - 1, 2)
                mul_b(p - 1, 2, nc.gpsimd if live else nc.vector, 2 if live else 1)
            if live:
                if ahead:
                    ti(p + 2, 0)
                    ic(p + 2, 0, nc.scalar.copy)
                mx_b(p, 1, 1)
                mx_b(p, 2, 0)
                mx_b(p, 2, 1)
                mask_b(p, 1)
                bias_b(p, 2)
                mask_b(p, 2)
                silu_b(p, 1)
                mul_b(p, 1, nc.gpsimd, 2)
                if ahead:
                    ti(p + 2, 1)
                    ic(p + 2, 1, nc.scalar.copy)
                to(p)
                oc(p)
